import numpy as np
import ml_dtypes


def mxq(x, axis, fmt="e4m3"):
    dtype, down = {"e4m3": (ml_dtypes.float8_e4m3fn, 7), "e5m2": (ml_dtypes.float8_e5m2, 14)}[fmt]
    v = np.moveaxis(np.asarray(x, np.float32).astype(ml_dtypes.bfloat16).astype(np.float64), axis, -1)
    blocks = v.reshape(v.shape[:-1] + (-1, 32))
    amax = np.abs(blocks).max(-1, keepdims=True)
    byte = np.maximum(np.where(amax > 0, np.frexp(amax)[1] - 1 + 127, 0) - down, 1)
    scale = np.exp2(byte - 127.0)
    codes = (blocks / scale).astype(np.float32).astype(dtype).astype(np.float64)
    return np.moveaxis((codes * scale).reshape(v.shape), -1, axis)


WIDE = False


def mx_kscale(k):
    if not WIDE:
        return np.ones(k)
    levels = np.array([10, -10, 5, -5, 0])
    if k % 512:
        return np.exp2(np.random.permutation(np.resize(levels, k // 32))).repeat(32)
    a = np.empty((k // 512, 16))
    for p in range(k // 512):
        a[p, :8] = np.random.permutation(np.resize(levels, 8))
        for g in range(8):
            far = levels[np.abs(levels - a[p, g]) >= 10]
            a[p, g + 8] = far[np.random.randint(len(far))]
    return np.exp2(a.ravel()).repeat(32)


BF16 = ml_dtypes.bfloat16


def bf(x):
    return np.asarray(x, np.float32).astype(BF16)


def f64(x):
    return np.asarray(x).astype(np.float64)


B, D, P, C, DEPTH = 4096, 1024, 512, 128, 2
INT = (1 << DEPTH) - 1
TOT = INT + INT + 1
SIGMA = 1.0


def path_probs(th):
    prob = np.ones((1, th.shape[1]))
    probs = [prob]
    off = 0
    for d in range(DEPTH):
        n = 1 << d
        t = th[off:off + n]
        left = prob * (1.0 + t) * 0.5
        right = prob * (1.0 - t) * 0.5
        prob = np.stack([left, right], axis=1).reshape(n + n, -1)
        probs.append(prob)
        off += n
    return np.concatenate(probs, axis=0)


def draw0():
    s, t = mx_kscale(D), mx_kscale(P)
    return {"X": bf(np.random.standard_normal((B, D)) * s),
            "Z": bf(np.random.standard_normal((P, D)) * 0.25 * P / np.sqrt(D) * t[:, None] / s),
            "W": bf(np.random.standard_normal((C * TOT, P)) * 4.0 / np.sqrt(P) / t),
            "V": bf(np.random.standard_normal((C * TOT, P)) * 4.0 / np.sqrt(P) / t),
            "th": bf(np.tanh(1.5 * np.random.standard_normal((INT, B))))}


def core(X, Z, W, V, th):
    Xp = (mxq(f64(Z), 1, "e4m3") @ mxq(f64(X), 1, "e4m3").T) / P
    Xq = mxq(Xp, 0, "e4m3")
    WX = (mxq(f64(W), 1, "e4m3") @ Xq).reshape(TOT, C, B)
    VX = (mxq(f64(V), 1, "e4m3") @ Xq).reshape(TOT, C, B)
    probs = path_probs(f64(th))
    return np.sum(probs[:, None, :] * WX * np.tanh(SIGMA * VX), axis=0)


def e4m3fn_bytes(y):
    return np.clip(np.asarray(y, np.float64), -448.0, 448.0).astype(np.float32).astype(ml_dtypes.float8_e4m3fn).view(np.uint8)


def e4m3fn_values(b):
    return np.asarray(b, np.uint8).view(ml_dtypes.float8_e4m3fn).astype(np.float64)


def setup_inputs():
    d = draw0()
    x0 = np.asarray(d['X']).astype(np.float64)
    s = (np.max(np.abs(x0), axis=(0,), keepdims=True) / 448.0).astype(np.float32)
    out = {}
    for k, v in d.items():
        if k == 'X':
            out['X_bytes'] = e4m3fn_bytes(x0 / s.astype(np.float64))
            out['X_scale'] = s
        else:
            out[k] = v
    return out


def reference(X_bytes, X_scale, Z, W, V, th):
    return core(e4m3fn_values(X_bytes) * X_scale.astype(np.float64), Z, W, V, th)

@@ -1,0 +1,284 @@
+from contextlib import ExitStack
+
+import concourse.mybir as mybir
+from concourse.masks import make_identity
+
+B, D, P, C, TOT = 4096, 1024, 512, 128, 7
+FLOPS = 2 * B * D * P + 2 * 2 * B * C * TOT * P
+
+F32 = mybir.dt.float32
+BF16 = mybir.dt.bfloat16
+U32 = mybir.dt.uint32
+U8 = mybir.dt.uint8
+FP8 = mybir.dt.float8_e4m3fn
+FP8X4 = mybir.dt.float8_e4m3fn_x4
+ACT = mybir.ActivationFunctionType
+ALU = mybir.AluOpType
+
+NPAIR = B // 256
+
+
+def tile_bonsailayer_pa_t_kernel(tc, X_bytes, X_scale, Z, W, V, th, out):
+    nc = tc.nc
+    with ExitStack() as ctx:
+        keep = ctx.enter_context(tc.tile_pool(name="keep", bufs=1))
+        work = ctx.enter_context(tc.tile_pool(name="work", bufs=2))
+        psum = ctx.enter_context(tc.psum_pool(name="psum", bufs=1))
+        ctx.enter_context(tc.manual_schedule())
+
+        def aux(shape, name):
+            return psum.tile(shape, F32, name=name, tag="aux", bufs=4)
+
+        warm = keep.tile([128, 1], F32, name="warm")
+        nc.vector.memset(warm[:], 0.0)
+        warm_out = keep.tile([128, 1], F32, name="warm_out")
+        scale = keep.tile([128, D], F32, name="scale")
+        nc.scalar.dma_start(out=scale[:], in_=X_scale.rearrange("o k -> (o k)").partition_broadcast(128))
+        nc.scalar.activation(out=warm_out[:], in_=warm[:], func=ACT.Tanh)
+
+        ident = keep.tile([128, 128], F32, name="ident")
+        make_identity(nc, ident[:])
+        th_rows = keep.tile([128, 256], BF16, name="th_rows")
+        nc.gpsimd.memset(th_rows[:], 0.0)
+        nc.scalar.dma_start(out=th_rows[0:48, :], in_=th.rearrange("i (j q) -> (i j) q", q=256))
+
+        z_sb = []
+        for g in range(2):
+            z_g = keep.tile([128, 4, 512], BF16, name="z_sb%d" % g)
+            nc.sync.dma_start(out=z_g[:], in_=Z.rearrange("(m t) k -> m t k", t=4)[:, :, 512 * g:512 * (g + 1)])
+            z_sb.append(z_g)
+        x_view = X_bytes.rearrange("(j p r) k -> j p (r k)", p=128, r=2)
+        x_bytes = []
+
+        def load_x(j):
+            xb = keep.tile([128, 2 * D], U8, name="xb%d" % j)
+            nc.sync.dma_start(out=xb[:], in_=x_view[j])
+            x_bytes.append(xb)
+
+        load_x(0)
+        v_sb = keep.tile([128, TOT, P], BF16, name="v_sb")
+        nc.sync.dma_start(out=v_sb[:], in_=V.rearrange("(n p) k -> p n k", p=128))
+        load_x(1)
+        w_sb = keep.tile([128, TOT, P], BF16, name="w_sb")
+        nc.sync.dma_start(out=w_sb[:], in_=W.rearrange("(n p) k -> p n k", p=128))
+        for j in range(2, NPAIR):
+            load_x(j)
+
+        th_f = keep.tile([128, 256], F32, name="th_f")
+        nc.gpsimd.tensor_copy(out=th_f[:], in_=th_rows[:])
+        left = keep.tile([128, 2, 48], F32, name="left")
+        right = keep.tile([128, 2, 48], F32, name="right")
+        probs = keep.tile([128, 4, 2, NPAIR], F32, name="probs")
+
+        def path_probabilities():
+            tp = aux([128, 2, 128], "tp")
+            for r in range(2):
+                nc.tensor.transpose(tp[:, r, :], th_f[:, r::2], ident[:])
+            nc.vector.tensor_scalar(out=left[:], in0=tp[:, :, 0:48], scalar1=0.5, scalar2=0.5, op0=ALU.mult, op1=ALU.add)
+            nc.vector.tensor_scalar(out=right[:], in0=tp[:, :, 0:48], scalar1=-0.5, scalar2=0.5, op0=ALU.mult, op1=ALU.add)
+            for c, (a, i, b) in enumerate(((left, 1, left), (left, 1, right), (right, 2, left), (right, 2, right))):
+                nc.gpsimd.tensor_tensor(out=probs[:, c], in0=a[:, :, 0:NPAIR], in1=b[:, :, NPAIR * i:NPAIR * (i + 1)], op=ALU.mult)
+
+        def prob(n, j, r):
+            if n in (1, 2):
+                t = left if n == 1 else right
+                return t[:, r, j:j + 1]
+            return probs[:, n - 3, r, j:j + 1]
+
+        z_codes = keep.tile([128, 2, P], U32, name="z_codes", align_bytes=64)
+        z_scales = keep.tile([128, 2, P], U8, name="z_scales", align_bytes=64)
+
+        def prep_z(g):
+            grouped = work.tile([128, P, 4], BF16, name="z_grouped", tag="wz_grouped", bufs=2, align_bytes=64)
+            gw = grouped[:].rearrange("p c t -> p (c t)").bitcast(F32).rearrange("p (c u) -> p c u", u=2)
+            words = z_sb[g][:].rearrange("m t k -> m (t k)").bitcast(F32)
+            for h in range(2):
+                bank = aux([128, 2, 2, 128], "zt")
+                for t in range(2):
+                    for u in range(2):
+                        lo = 256 * (2 * h + t)
+                        nc.tensor.transpose(bank[:, t, u, :], words[:, lo + u:lo + 256:2], ident[:])
+                dst = gw[:, 256 * h:256 * (h + 1), :].rearrange("p (t m) u -> p t m u", t=2)
+                src = bank[:].rearrange("p t u m -> p t m u")
+                if h == 0:
+                    nc.scalar.copy(out=dst, in_=src)
+                else:
+                    nc.vector.tensor_copy(out=dst, in_=src)
+            nc.vector.quantize_mx(out=z_codes[:, g, :].bitcast(FP8X4), scales=z_scales[:, g, :],
+                                  in_=grouped[:].rearrange("p c t -> p (c t)"))
+
+        v_codes = keep.tile([128, TOT * C], U32, name="v_codes", align_bytes=64)
+        v_scales = keep.tile([128, TOT * C], U8, name="v_scales", align_bytes=64)
+        w_codes = keep.tile([128, TOT * C], U32, name="w_codes", align_bytes=64)
+        w_scales = keep.tile([128, TOT * C], U8, name="w_scales", align_bytes=64)
+
+        def prep_w(sb, codes, scales):
+            words = sb[:].rearrange("p n k -> p (n k)").bitcast(F32)
+            for n0, nn in ((0, 4), (4, 2), (6, 1)):
+                grouped = work.tile([128, 512, 4], BF16, name="w_grouped", tag="wz_grouped", bufs=2, align_bytes=64)
+                flat = grouped[:].rearrange("p c t -> p (c t)")[:, 0:512 * nn]
+                gw = flat.bitcast(F32).rearrange("p (c u) -> p c u", u=2)
+                for h0 in range(0, nn, 2):
+                    hn = min(2, nn - h0)
+                    bank = aux([128, 2, 2, 128], "wt")
+                    for a in range(hn):
+                        for u in range(2):
+                            lo = 256 * (n0 + h0 + a)
+                            nc.tensor.transpose(bank[:, a, u, :], words[:, lo + u:lo + 256:2], ident[:])
+                    dst = gw[:, 128 * h0:128 * (h0 + hn), :].rearrange("p (a c) u -> p a c u", a=hn)
+                    src = bank[:, 0:hn].rearrange("p a u c -> p a c u")
+                    if (n0 + h0) % 4 == 0:
+                        nc.scalar.copy(out=dst, in_=src)
+                    else:
+                        nc.vector.tensor_copy(out=dst, in_=src)
+                cols = slice(128 * n0, 128 * (n0 + nn))
+                nc.vector.quantize_mx(out=codes[:, cols].bitcast(FP8X4), scales=scales[:, cols], in_=flat)
+
+        xs, xt, xg, xq, yb, yg, yq, gate, prod, acc = {}, {}, {}, {}, {}, {}, {}, {}, {}, {}
+
+        def stage_p(j, h):
+            if h == 0:
+                xs[j] = work.tile([128, 2 * D], BF16, name="xs", tag="xs", bufs=3, align_bytes=64)
+            lo = 512 * h
+            k0 = lo % D
+            nc.vector.tensor_tensor(out=xs[j][:, lo:lo + 512], in0=x_bytes[j][:, lo:lo + 512].bitcast(FP8),
+                                    in1=scale[:, k0:k0 + 512], op=ALU.mult)
+
+        def stage_t(j):
+            words = xs[j][:].bitcast(F32)
+            for r in range(2):
+                bank = aux([128, 2, 2, 128], "xt")
+                for g in range(2):
+                    for u in range(2):
+                        lo = 512 * r + 256 * g
+                        nc.tensor.transpose(bank[:, g, u, :], words[:, lo + u:lo + 256:2], ident[:])
+                xt[j, r] = bank
+
+        def stage_c(j):
+            xg[j] = work.tile([128, 2, 2, 128, 4], BF16, name="xg", tag="xg", bufs=2, align_bytes=64)
+            w = xg[j][:].rearrange("p r g b t -> p (r g b t)").bitcast(F32).rearrange("p (r g b u) -> p r g b u", r=2, g=2, u=2)
+            for r in range(2):
+                nc.scalar.copy(out=w[:, r], in_=xt[j, r][:].rearrange("p g u b -> p g b u"))
+
+        def stage_q(j):
+            codes = work.tile([128, 512], U32, name="xq", tag="xq", bufs=3, align_bytes=64)
+            scales = work.tile([128, 512], U8, name="xqs", tag="xqs", bufs=3, align_bytes=64)
+            nc.vector.quantize_mx(out=codes[:].bitcast(FP8X4), scales=scales[:],
+                                  in_=xg[j][:].rearrange("p r g b t -> p (r g b t)"))
+            xq[j] = (codes, scales)
+
+        def stage_m1(j):
+            codes, scales = xq[j]
+            for r in range(2):
+                bank = aux([128, 4, 128], "yb")
+                for t in range(4):
+                    for g in range(2):
+                        cols = slice(128 * (2 * r + g), 128 * (2 * r + g + 1))
+                        nc.tensor.matmul_mx(out=bank[:, t, :],
+                                            lhsT=z_codes[:, g, 128 * t:128 * (t + 1)].bitcast(FP8X4),
+                                            lhsT_scale=z_scales[:, g, 128 * t:128 * (t + 1)],
+                                            rhs=codes[:, cols].bitcast(FP8X4), rhs_scale=scales[:, cols],
+                                            start=(g == 0), stop=(g == 1))
+                yb[j, r] = bank
+
+        def stage_e(j):
+            yg[j] = work.tile([128, 2, 128, 4], BF16, name="yg", tag="yg", bufs=2, align_bytes=64)
+            for r in range(2):
+                nc.scalar.activation(out=yg[j][:, r], in_=yb[j, r][:].rearrange("p t b -> p b t"), func=ACT.Copy, scale=1.0 / P)
+
+        def stage_q2(j):
+            codes = work.tile([128, 256], U32, name="yq", tag="yq", bufs=3, align_bytes=64)
+            scales = work.tile([128, 256], U8, name="yqs", tag="yqs", bufs=3, align_bytes=64)
+            nc.vector.quantize_mx(out=codes[:].bitcast(FP8X4), scales=scales[:],
+                                  in_=yg[j][:].rearrange("p r b t -> p (r b t)"))
+            yq[j] = (codes, scales)
+
+        mm = {}
+
+        def stage_m2(j, r):
+            codes, scales = yq[j]
+            cols = slice(128 * r, 128 * (r + 1))
+            for side, (wc, ws) in (("v", (v_codes, v_scales)), ("w", (w_codes, w_scales))):
+                low = psum.tile([128, 512], F32, name=side + "_low", tag=side + "_low", bufs=1)
+                high = psum.tile([128, 384], F32, name=side + "_high", tag=side + "_high", bufs=1)
+                for dst, c0, c1 in ((low[:], 0, 512), (high[:, 0:256], 512, 768), (high[:, 256:384], 768, 896)):
+                    nc.tensor.matmul_mx(out=dst, lhsT=codes[:, cols].bitcast(FP8X4), lhsT_scale=scales[:, cols],
+                                        rhs=wc[:, c0:c1].bitcast(FP8X4), rhs_scale=ws[:, c0:c1], start=True, stop=True)
+                mm[side] = (low, high)
+
+        def stage_h(j, r):
+            g = work.tile([128, TOT * C], F32, name="gate", tag="gate", bufs=3)
+            low, high = mm["v"]
+            nc.scalar.activation(out=g[:, 0:512], in_=low[:], func=ACT.Tanh)
+            nc.scalar.activation(out=g[:, 512:896], in_=high[:], func=ACT.Tanh)
+            gate[j, r] = g
+
+        def stage_s(j, r):
+            pr = work.tile([128, TOT, C], F32, name="prod", tag="prod%d" % r, bufs=2)
+            low, high = mm["w"]
+            for n in range(TOT):
+                src = low[:, 128 * n:128 * (n + 1)] if n < 4 else high[:, 128 * (n - 4):128 * (n - 3)]
+                g = gate[j, r][:, 128 * n:128 * (n + 1)]
+                if n == 0:
+                    nc.vector.tensor_tensor(out=pr[:, n, :], in0=src, in1=g, op=ALU.mult)
+                else:
+                    nc.vector.scalar_tensor_tensor(out=pr[:, n, :], in0=src, scalar=prob(n, j, r), in1=g,
+                                                   op0=ALU.mult, op1=ALU.mult)
+            prod[j, r] = pr
+
+        def stage_a(j):
+            bank = aux([128, 2, 128], "acc")
+            for r in range(2):
+                for n in range(TOT):
+                    nc.tensor.matmul(out=bank[:, r, :], lhsT=prod[j, r][:, n, :], rhs=ident[:],
+                                     start=(n == 0), stop=(n == TOT - 1), is_transpose=True)
+            acc[j] = bank
+
+        def stage_f(j):
+            o = work.tile([128, 128, 2], F32, name="o", tag="o", bufs=3)
+            nc.scalar.copy(out=o[:], in_=acc[j][:].rearrange("c r p -> c p r"))
+            nc.sync.dma_start(out=out[:, 256 * j:256 * (j + 1)], in_=o[:].rearrange("c p r -> c (p r)"))
+
+        def ok(j):
+            return 0 <= j < NPAIR
+
+        for g in range(2):
+            prep_z(g)
+        path_probabilities()
+        for j in range(-4, NPAIR + 1):
+            if ok(j):
+                stage_m2(j, 0)
+                stage_h(j, 0)
+            if ok(j + 4):
+                stage_p(j + 4, 0)
+                stage_p(j + 4, 1)
+            if ok(j):
+                stage_s(j, 0)
+            if ok(j + 3):
+                stage_t(j + 3)
+            if ok(j + 1):
+                stage_e(j + 1)
+            if ok(j + 4):
+                stage_p(j + 4, 2)
+            if ok(j + 1):
+                stage_q2(j + 1)
+            if ok(j - 1):
+                stage_a(j - 1)
+            if ok(j + 3):
+                stage_c(j + 3)
+            if ok(j + 4):
+                stage_p(j + 4, 3)
+            if ok(j - 1):
+                stage_f(j - 1)
+            if ok(j + 3):
+                stage_q(j + 3)
+            if j == -3:
+                prep_w(v_sb, v_codes, v_scales)
+            if j == -2:
+                prep_w(w_sb, w_codes, w_scales)
+            if ok(j):
+                stage_m2(j, 1)
+                stage_h(j, 1)
+                stage_s(j, 1)
+            if ok(j + 2):
+                stage_m1(j + 2)

@@ -112,9 +112,9 @@ def tile_bonsailayer_pa_t_kernel(tc, X_bytes, X_scale, Z, W, V, th, out):
         w_codes = keep.tile([128, TOT * C], U32, name="w_codes", align_bytes=64)
         w_scales = keep.tile([128, TOT * C], U8, name="w_scales", align_bytes=64)
 
-        def prep_w(sb, codes, scales):
+        def prep_w(sb, codes, scales, chunks):
             words = sb[:].rearrange("p n k -> p (n k)").bitcast(F32)
-            for n0, nn in ((0, 4), (4, 2), (6, 1)):
+            for n0, nn in chunks:
                 grouped = work.tile([128, 512, 4], BF16, name="w_grouped", tag="wz_grouped", bufs=2, align_bytes=64)
                 flat = grouped[:].rearrange("p c t -> p (c t)")[:, 0:512 * nn]
                 gw = flat.bitcast(F32).rearrange("p (c u) -> p c u", u=2)
@@ -134,151 +134,136 @@ def tile_bonsailayer_pa_t_kernel(tc, X_bytes, X_scale, Z, W, V, th, out):
                 cols = slice(128 * n0, 128 * (n0 + nn))
                 nc.vector.quantize_mx(out=codes[:, cols].bitcast(FP8X4), scales=scales[:, cols], in_=flat)
 
-        xs, xt, xg, xq, yb, yg, yq, gate, prod, acc = {}, {}, {}, {}, {}, {}, {}, {}, {}, {}
+        xs, xt, xg, xq, yb, yg, yq, gate, prod, acc, mm = {}, {}, {}, {}, {}, {}, {}, {}, {}, {}, {}
 
-        def stage_p(j, h):
-            if h == 0:
-                xs[j] = work.tile([128, 2 * D], BF16, name="xs", tag="xs", bufs=3, align_bytes=64)
-            lo = 512 * h
-            k0 = lo % D
-            nc.vector.tensor_tensor(out=xs[j][:, lo:lo + 512], in0=x_bytes[j][:, lo:lo + 512].bitcast(FP8),
-                                    in1=scale[:, k0:k0 + 512], op=ALU.mult)
+        def stage_p(i):
+            j, r = divmod(i, 2)
+            xs[i] = work.tile([128, D], BF16, name="xs", tag="xs", bufs=4, align_bytes=64)
+            nc.vector.tensor_tensor(out=xs[i][:], in0=x_bytes[j][:, D * r:D * (r + 1)].bitcast(FP8), in1=scale[:], op=ALU.mult)
 
-        def stage_t(j):
-            words = xs[j][:].bitcast(F32)
-            for r in range(2):
-                bank = aux([128, 2, 2, 128], "xt")
+        def stage_t(i):
+            words = xs[i][:].bitcast(F32)
+            bank = aux([128, 2, 2, 128], "xt")
+            for g in range(2):
+                for u in range(2):
+                    nc.tensor.transpose(bank[:, g, u, :], words[:, 256 * g + u:256 * (g + 1):2], ident[:])
+            xt[i] = bank
+
+        def stage_c(i):
+            xg[i] = work.tile([128, 2, 128, 4], BF16, name="xg", tag="xg", bufs=3, align_bytes=64)
+            w = xg[i][:].rearrange("p g b t -> p (g b t)").bitcast(F32).rearrange("p (g b u) -> p g b u", g=2, u=2)
+            nc.scalar.copy(out=w, in_=xt[i][:].rearrange("p g u b -> p g b u"))
+
+        def stage_q(i):
+            codes = work.tile([128, 256], U32, name="xq", tag="xq", bufs=3, align_bytes=64)
+            scales = work.tile([128, 256], U8, name="xqs", tag="xqs", bufs=3, align_bytes=64)
+            nc.vector.quantize_mx(out=codes[:].bitcast(FP8X4), scales=scales[:],
+                                  in_=xg[i][:].rearrange("p g b t -> p (g b t)"))
+            xq[i] = (codes, scales)
+
+        def stage_m1(i):
+            codes, scales = xq[i]
+            bank = aux([128, 4, 128], "yb")
+            for t in range(4):
                 for g in range(2):
-                    for u in range(2):
-                        lo = 512 * r + 256 * g
-                        nc.tensor.transpose(bank[:, g, u, :], words[:, lo + u:lo + 256:2], ident[:])
-                xt[j, r] = bank
+                    cols = slice(128 * g, 128 * (g + 1))
+                    nc.tensor.matmul_mx(out=bank[:, t, :],
+                                        lhsT=z_codes[:, g, 128 * t:128 * (t + 1)].bitcast(FP8X4),
+                                        lhsT_scale=z_scales[:, g, 128 * t:128 * (t + 1)],
+                                        rhs=codes[:, cols].bitcast(FP8X4), rhs_scale=scales[:, cols],
+                                        start=(g == 0), stop=(g == 1))
+            yb[i] = bank
 
-        def stage_c(j):
-            xg[j] = work.tile([128, 2, 2, 128, 4], BF16, name="xg", tag="xg", bufs=2, align_bytes=64)
-            w = xg[j][:].rearrange("p r g b t -> p (r g b t)").bitcast(F32).rearrange("p (r g b u) -> p r g b u", r=2, g=2, u=2)
-            for r in range(2):
-                nc.scalar.copy(out=w[:, r], in_=xt[j, r][:].rearrange("p g u b -> p g b u"))
+        def stage_e(i):
+            yg[i] = work.tile([128, 128, 4], BF16, name="yg", tag="yg", bufs=3, align_bytes=64)
+            nc.scalar.activation(out=yg[i][:], in_=yb[i][:].rearrange("p t b -> p b t"), func=ACT.Copy, scale=1.0 / P)
 
-        def stage_q(j):
-            codes = work.tile([128, 512], U32, name="xq", tag="xq", bufs=3, align_bytes=64)
-            scales = work.tile([128, 512], U8, name="xqs", tag="xqs", bufs=3, align_bytes=64)
-            nc.vector.quantize_mx(out=codes[:].bitcast(FP8X4), scales=scales[:],
-                                  in_=xg[j][:].rearrange("p r g b t -> p (r g b t)"))
-            xq[j] = (codes, scales)
+        def stage_q2(i):
+            codes = work.tile([128, 128], U32, name="yq", tag="yq", bufs=3, align_bytes=64)
+            scales = work.tile([128, 128], U8, name="yqs", tag="yqs", bufs=3, align_bytes=64)
+            nc.vector.quantize_mx(out=codes[:].bitcast(FP8X4), scales=scales[:], in_=yg[i][:].rearrange("p b t -> p (b t)"))
+            yq[i] = (codes, scales)
 
-        def stage_m1(j):
-            codes, scales = xq[j]
-            for r in range(2):
-                bank = aux([128, 4, 128], "yb")
-                for t in range(4):
-                    for g in range(2):
-                        cols = slice(128 * (2 * r + g), 128 * (2 * r + g + 1))
-                        nc.tensor.matmul_mx(out=bank[:, t, :],
-                                            lhsT=z_codes[:, g, 128 * t:128 * (t + 1)].bitcast(FP8X4),
-                                            lhsT_scale=z_scales[:, g, 128 * t:128 * (t + 1)],
-                                            rhs=codes[:, cols].bitcast(FP8X4), rhs_scale=scales[:, cols],
-                                            start=(g == 0), stop=(g == 1))
-                yb[j, r] = bank
-
-        def stage_e(j):
-            yg[j] = work.tile([128, 2, 128, 4], BF16, name="yg", tag="yg", bufs=2, align_bytes=64)
-            for r in range(2):
-                nc.scalar.activation(out=yg[j][:, r], in_=yb[j, r][:].rearrange("p t b -> p b t"), func=ACT.Copy, scale=1.0 / P)
-
-        def stage_q2(j):
-            codes = work.tile([128, 256], U32, name="yq", tag="yq", bufs=3, align_bytes=64)
-            scales = work.tile([128, 256], U8, name="yqs", tag="yqs", bufs=3, align_bytes=64)
-            nc.vector.quantize_mx(out=codes[:].bitcast(FP8X4), scales=scales[:],
-                                  in_=yg[j][:].rearrange("p r b t -> p (r b t)"))
-            yq[j] = (codes, scales)
-
-        mm = {}
-
-        def stage_m2(j, r):
-            codes, scales = yq[j]
-            cols = slice(128 * r, 128 * (r + 1))
+        def stage_m2(i):
+            codes, scales = yq[i]
             for side, (wc, ws) in (("v", (v_codes, v_scales)), ("w", (w_codes, w_scales))):
                 low = psum.tile([128, 512], F32, name=side + "_low", tag=side + "_low", bufs=1)
                 high = psum.tile([128, 384], F32, name=side + "_high", tag=side + "_high", bufs=1)
                 for dst, c0, c1 in ((low[:], 0, 512), (high[:, 0:256], 512, 768), (high[:, 256:384], 768, 896)):
-                    nc.tensor.matmul_mx(out=dst, lhsT=codes[:, cols].bitcast(FP8X4), lhsT_scale=scales[:, cols],
+                    nc.tensor.matmul_mx(out=dst, lhsT=codes[:].bitcast(FP8X4), lhsT_scale=scales[:],
                                         rhs=wc[:, c0:c1].bitcast(FP8X4), rhs_scale=ws[:, c0:c1], start=True, stop=True)
                 mm[side] = (low, high)
 
-        def stage_h(j, r):
+        def stage_h(i):
             g = work.tile([128, TOT * C], F32, name="gate", tag="gate", bufs=3)
             low, high = mm["v"]
             nc.scalar.activation(out=g[:, 0:512], in_=low[:], func=ACT.Tanh)
             nc.scalar.activation(out=g[:, 512:896], in_=high[:], func=ACT.Tanh)
-            gate[j, r] = g
+            gate[i] = g
 
-        def stage_s(j, r):
-            pr = work.tile([128, TOT, C], F32, name="prod", tag="prod%d" % r, bufs=2)
+        def stage_s(i):
+            j, r = divmod(i, 2)
+            pr = work.tile([128, TOT, C], F32, name="prod", tag="prod", bufs=3)
             low, high = mm["w"]
             for n in range(TOT):
                 src = low[:, 128 * n:128 * (n + 1)] if n < 4 else high[:, 128 * (n - 4):128 * (n - 3)]
-                g = gate[j, r][:, 128 * n:128 * (n + 1)]
+                g = gate[i][:, 128 * n:128 * (n + 1)]
                 if n == 0:
                     nc.vector.tensor_tensor(out=pr[:, n, :], in0=src, in1=g, op=ALU.mult)
                 else:
                     nc.vector.scalar_tensor_tensor(out=pr[:, n, :], in0=src, scalar=prob(n, j, r), in1=g,
                                                    op0=ALU.mult, op1=ALU.mult)
-            prod[j, r] = pr
+            prod[i] = pr
 
-        def stage_a(j):
-            bank = aux([128, 2, 128], "acc")
-            for r in range(2):
-                for n in range(TOT):
-                    nc.tensor.matmul(out=bank[:, r, :], lhsT=prod[j, r][:, n, :], rhs=ident[:],
-                                     start=(n == 0), stop=(n == TOT - 1), is_transpose=True)
-            acc[j] = bank
+        def stage_a(i):
+            j, r = divmod(i, 2)
+            if r == 0:
+                acc[j] = aux([128, 2, 128], "acc")
+            for n in range(TOT):
+                nc.tensor.matmul(out=acc[j][:, r, :], lhsT=prod[i][:, n, :], rhs=ident[:],
+                                 start=(n == 0), stop=(n == TOT - 1), is_transpose=True)
 
         def stage_f(j):
             o = work.tile([128, 128, 2], F32, name="o", tag="o", bufs=3)
             nc.scalar.copy(out=o[:], in_=acc[j][:].rearrange("c r p -> c p r"))
             nc.sync.dma_start(out=out[:, 256 * j:256 * (j + 1)], in_=o[:].rearrange("c p r -> c (p r)"))
 
-        def ok(j):
-            return 0 <= j < NPAIR
+        def ok(i):
+            return 0 <= i < 2 * NPAIR
 
         for g in range(2):
             prep_z(g)
         path_probabilities()
-        for j in range(-4, NPAIR + 1):
-            if ok(j):
-                stage_m2(j, 0)
-                stage_h(j, 0)
-            if ok(j + 4):
-                stage_p(j + 4, 0)
-                stage_p(j + 4, 1)
-            if ok(j):
-                stage_s(j, 0)
-            if ok(j + 3):
-                stage_t(j + 3)
-            if ok(j + 1):
-                stage_e(j + 1)
-            if ok(j + 4):
-                stage_p(j + 4, 2)
-            if ok(j + 1):
-                stage_q2(j + 1)
-            if ok(j - 1):
-                stage_a(j - 1)
-            if ok(j + 3):
-                stage_c(j + 3)
-            if ok(j + 4):
-                stage_p(j + 4, 3)
-            if ok(j - 1):
-                stage_f(j - 1)
-            if ok(j + 3):
-                stage_q(j + 3)
-            if j == -3:
-                prep_w(v_sb, v_codes, v_scales)
-            if j == -2:
-                prep_w(w_sb, w_codes, w_scales)
-            if ok(j):
-                stage_m2(j, 1)
-                stage_h(j, 1)
-                stage_s(j, 1)
-            if ok(j + 2):
-                stage_m1(j + 2)
+        for i in range(-4, 2 * NPAIR + 1):
+            if ok(i):
+                stage_m2(i)
+            if ok(i + 1):
+                stage_e(i + 1)
+            if ok(i):
+                stage_h(i)
+            if ok(i + 2):
+                stage_q(i + 2)
+            if ok(i + 4):
+                stage_p(i + 4)
+            if ok(i + 1):
+                stage_q2(i + 1)
+            if ok(i + 3):
+                stage_t(i + 3)
+            if ok(i - 1):
+                stage_a(i - 1)
+            if i == -4:
+                prep_w(v_sb, v_codes, v_scales, ((0, 4),))
+            if i == -3:
+                prep_w(v_sb, v_codes, v_scales, ((4, 2), (6, 1)))
+            if i == -2:
+                prep_w(w_sb, w_codes, w_scales, ((0, 4),))
+            if i == -1:
+                prep_w(w_sb, w_codes, w_scales, ((4, 2), (6, 1)))
+            if ok(i):
+                stage_s(i)
+            if ok(i + 3):
+                stage_c(i + 3)
+            if ok(i - 1) and i % 2 == 0:
+                stage_f((i - 1) // 2)
+            if ok(i + 2):
+                stage_m1(i + 2)

from contextlib import ExitStack

import concourse.mybir as mybir
from concourse.masks import make_identity

B, D, P, C, TOT = 4096, 1024, 512, 128, 7
FLOPS = 2 * B * D * P + 2 * 2 * B * C * TOT * P

F32 = mybir.dt.float32
BF16 = mybir.dt.bfloat16
U32 = mybir.dt.uint32
U8 = mybir.dt.uint8
FP8 = mybir.dt.float8_e4m3fn
FP8X4 = mybir.dt.float8_e4m3fn_x4
ACT = mybir.ActivationFunctionType
ALU = mybir.AluOpType

NPAIR = B // 256


def tile_bonsailayer_pa_t_kernel(tc, X_bytes, X_scale, Z, W, V, th, out):
    nc = tc.nc
    with ExitStack() as ctx:
        keep = ctx.enter_context(tc.tile_pool(name="keep", bufs=1))
        work = ctx.enter_context(tc.tile_pool(name="work", bufs=2))
        psum = ctx.enter_context(tc.psum_pool(name="psum", bufs=1))
        ctx.enter_context(tc.manual_schedule())

        def aux(shape, name):
            return psum.tile(shape, F32, name=name, tag="aux", bufs=4)

        warm = keep.tile([128, 1], F32, name="warm")
        nc.vector.memset(warm[:], 0.0)
        warm_out = keep.tile([128, 1], F32, name="warm_out")
        scale = keep.tile([128, D], F32, name="scale")
        nc.scalar.dma_start(out=scale[:], in_=X_scale.rearrange("o k -> (o k)").partition_broadcast(128))
        nc.scalar.activation(out=warm_out[:], in_=warm[:], func=ACT.Tanh)

        ident = keep.tile([128, 128], F32, name="ident")
        make_identity(nc, ident[:])
        th_rows = keep.tile([128, 256], BF16, name="th_rows")
        nc.gpsimd.memset(th_rows[:], 0.0)
        nc.scalar.dma_start(out=th_rows[0:48, :], in_=th.rearrange("i (j q) -> (i j) q", q=256))

        z_sb = []
        for g in range(2):
            z_g = keep.tile([128, 4, 512], BF16, name="z_sb%d" % g)
            nc.sync.dma_start(out=z_g[:], in_=Z.rearrange("(m t) k -> m t k", t=4)[:, :, 512 * g:512 * (g + 1)])
            z_sb.append(z_g)
        x_view = X_bytes.rearrange("(j p r) k -> j p (r k)", p=128, r=2)
        x_bytes = []

        def load_x(j):
            xb = keep.tile([128, 2 * D], U8, name="xb%d" % j)
            nc.sync.dma_start(out=xb[:], in_=x_view[j])
            x_bytes.append(xb)

        load_x(0)
        v_sb = keep.tile([128, TOT, P], BF16, name="v_sb")
        nc.sync.dma_start(out=v_sb[:], in_=V.rearrange("(n p) k -> p n k", p=128))
        load_x(1)
        w_sb = keep.tile([128, TOT, P], BF16, name="w_sb")
        nc.sync.dma_start(out=w_sb[:], in_=W.rearrange("(n p) k -> p n k", p=128))
        for j in range(2, NPAIR):
            load_x(j)

        th_f = keep.tile([128, 256], F32, name="th_f")
        nc.gpsimd.tensor_copy(out=th_f[:], in_=th_rows[:])
        left = keep.tile([128, 2, 48], F32, name="left")
        right = keep.tile([128, 2, 48], F32, name="right")
        probs = keep.tile([128, 4, 2, NPAIR], F32, name="probs")

        def path_probabilities():
            tp = aux([128, 2, 128], "tp")
            for r in range(2):
                nc.tensor.transpose(tp[:, r, :], th_f[:, r::2], ident[:])
            nc.vector.tensor_scalar(out=left[:], in0=tp[:, :, 0:48], scalar1=0.5, scalar2=0.5, op0=ALU.mult, op1=ALU.add)
            nc.vector.tensor_scalar(out=right[:], in0=tp[:, :, 0:48], scalar1=-0.5, scalar2=0.5, op0=ALU.mult, op1=ALU.add)
            for c, (a, i, b) in enumerate(((left, 1, left), (left, 1, right), (right, 2, left), (right, 2, right))):
                nc.gpsimd.tensor_tensor(out=probs[:, c], in0=a[:, :, 0:NPAIR], in1=b[:, :, NPAIR * i:NPAIR * (i + 1)], op=ALU.mult)

        def prob(n, j, r):
            if n in (1, 2):
                t = left if n == 1 else right
                return t[:, r, j:j + 1]
            return probs[:, n - 3, r, j:j + 1]

        z_codes = keep.tile([128, 2, P], U32, name="z_codes", align_bytes=64)
        z_scales = keep.tile([128, 2, P], U8, name="z_scales", align_bytes=64)

        def prep_z(g):
            grouped = work.tile([128, P, 4], BF16, name="z_grouped", tag="wz_grouped", bufs=2, align_bytes=64)
            gw = grouped[:].rearrange("p c t -> p (c t)").bitcast(F32).rearrange("p (c u) -> p c u", u=2)
            words = z_sb[g][:].rearrange("m t k -> m (t k)").bitcast(F32)
            for h in range(2):
                bank = aux([128, 2, 2, 128], "zt")
                for t in range(2):
                    for u in range(2):
                        lo = 256 * (2 * h + t)
                        nc.tensor.transpose(bank[:, t, u, :], words[:, lo + u:lo + 256:2], ident[:])
                dst = gw[:, 256 * h:256 * (h + 1), :].rearrange("p (t m) u -> p t m u", t=2)
                src = bank[:].rearrange("p t u m -> p t m u")
                if h == 0:
                    nc.scalar.copy(out=dst, in_=src)
                else:
                    nc.vector.tensor_copy(out=dst, in_=src)
            nc.vector.quantize_mx(out=z_codes[:, g, :].bitcast(FP8X4), scales=z_scales[:, g, :],
                                  in_=grouped[:].rearrange("p c t -> p (c t)"))

        v_codes = keep.tile([128, TOT * C], U32, name="v_codes", align_bytes=64)
        v_scales = keep.tile([128, TOT * C], U8, name="v_scales", align_bytes=64)
        w_codes = keep.tile([128, TOT * C], U32, name="w_codes", align_bytes=64)
        w_scales = keep.tile([128, TOT * C], U8, name="w_scales", align_bytes=64)

        def prep_w(sb, codes, scales, chunks):
            words = sb[:].rearrange("p n k -> p (n k)").bitcast(F32)
            for n0, nn in chunks:
                grouped = work.tile([128, 512, 4], BF16, name="w_grouped", tag="wz_grouped", bufs=2, align_bytes=64)
                flat = grouped[:].rearrange("p c t -> p (c t)")[:, 0:512 * nn]
                gw = flat.bitcast(F32).rearrange("p (c u) -> p c u", u=2)
                for h0 in range(0, nn, 2):
                    hn = min(2, nn - h0)
                    bank = aux([128, 2, 2, 128], "wt")
                    for a in range(hn):
                        for u in range(2):
                            lo = 256 * (n0 + h0 + a)
                            nc.tensor.transpose(bank[:, a, u, :], words[:, lo + u:lo + 256:2], ident[:])
                    dst = gw[:, 128 * h0:128 * (h0 + hn), :].rearrange("p (a c) u -> p a c u", a=hn)
                    src = bank[:, 0:hn].rearrange("p a u c -> p a c u")
                    if (n0 + h0) % 4 == 0:
                        nc.scalar.copy(out=dst, in_=src)
                    else:
                        nc.vector.tensor_copy(out=dst, in_=src)
                cols = slice(128 * n0, 128 * (n0 + nn))
                nc.vector.quantize_mx(out=codes[:, cols].bitcast(FP8X4), scales=scales[:, cols], in_=flat)

        xs, xt, xg, xq, yb, yg, yq, gate, prod, acc, mm = {}, {}, {}, {}, {}, {}, {}, {}, {}, {}, {}

        def stage_p(i):
            j, r = divmod(i, 2)
            xs[i] = work.tile([128, D], BF16, name="xs", tag="xs", bufs=4, align_bytes=64)
            nc.vector.tensor_tensor(out=xs[i][:], in0=x_bytes[j][:, D * r:D * (r + 1)].bitcast(FP8), in1=scale[:], op=ALU.mult)

        def stage_t(i):
            words = xs[i][:].bitcast(F32)
            bank = aux([128, 2, 2, 128], "xt")
            for g in range(2):
                for u in range(2):
                    nc.tensor.transpose(bank[:, g, u, :], words[:, 256 * g + u:256 * (g + 1):2], ident[:])
            xt[i] = bank

        def stage_c(i):
            xg[i] = work.tile([128, 2, 128, 4], BF16, name="xg", tag="xg", bufs=3, align_bytes=64)
            w = xg[i][:].rearrange("p g b t -> p (g b t)").bitcast(F32).rearrange("p (g b u) -> p g b u", g=2, u=2)
            nc.scalar.copy(out=w, in_=xt[i][:].rearrange("p g u b -> p g b u"))

        def stage_q(i):
            codes = work.tile([128, 256], U32, name="xq", tag="xq", bufs=3, align_bytes=64)
            scales = work.tile([128, 256], U8, name="xqs", tag="xqs", bufs=3, align_bytes=64)
            nc.vector.quantize_mx(out=codes[:].bitcast(FP8X4), scales=scales[:],
                                  in_=xg[i][:].rearrange("p g b t -> p (g b t)"))
            xq[i] = (codes, scales)

        def stage_m1(i):
            codes, scales = xq[i]
            bank = aux([128, 4, 128], "yb")
            for t in range(4):
                for g in range(2):
                    cols = slice(128 * g, 128 * (g + 1))
                    nc.tensor.matmul_mx(out=bank[:, t, :],
                                        lhsT=z_codes[:, g, 128 * t:128 * (t + 1)].bitcast(FP8X4),
                                        lhsT_scale=z_scales[:, g, 128 * t:128 * (t + 1)],
                                        rhs=codes[:, cols].bitcast(FP8X4), rhs_scale=scales[:, cols],
                                        start=(g == 0), stop=(g == 1))
            yb[i] = bank

        def stage_e(i):
            yg[i] = work.tile([128, 128, 4], BF16, name="yg", tag="yg", bufs=3, align_bytes=64)
            nc.scalar.activation(out=yg[i][:], in_=yb[i][:].rearrange("p t b -> p b t"), func=ACT.Copy, scale=1.0 / P)

        def stage_q2(i):
            codes = work.tile([128, 128], U32, name="yq", tag="yq", bufs=3, align_bytes=64)
            scales = work.tile([128, 128], U8, name="yqs", tag="yqs", bufs=3, align_bytes=64)
            nc.vector.quantize_mx(out=codes[:].bitcast(FP8X4), scales=scales[:], in_=yg[i][:].rearrange("p b t -> p (b t)"))
            yq[i] = (codes, scales)

        def stage_m2(i):
            codes, scales = yq[i]
            for side, (wc, ws) in (("v", (v_codes, v_scales)), ("w", (w_codes, w_scales))):
                low = psum.tile([128, 512], F32, name=side + "_low", tag=side + "_low", bufs=1)
                high = psum.tile([128, 384], F32, name=side + "_high", tag=side + "_high", bufs=1)
                for dst, c0, c1 in ((low[:], 0, 512), (high[:, 0:256], 512, 768), (high[:, 256:384], 768, 896)):
                    nc.tensor.matmul_mx(out=dst, lhsT=codes[:].bitcast(FP8X4), lhsT_scale=scales[:],
                                        rhs=wc[:, c0:c1].bitcast(FP8X4), rhs_scale=ws[:, c0:c1], start=True, stop=True)
                mm[side] = (low, high)

        def stage_h(i):
            g = work.tile([128, TOT * C], F32, name="gate", tag="gate", bufs=3)
            low, high = mm["v"]
            nc.scalar.activation(out=g[:, 0:512], in_=low[:], func=ACT.Tanh)
            nc.scalar.activation(out=g[:, 512:896], in_=high[:], func=ACT.Tanh)
            gate[i] = g

        def stage_s(i):
            j, r = divmod(i, 2)
            pr = work.tile([128, TOT, C], F32, name="prod", tag="prod", bufs=3)
            low, high = mm["w"]
            for n in range(TOT):
                src = low[:, 128 * n:128 * (n + 1)] if n < 4 else high[:, 128 * (n - 4):128 * (n - 3)]
                g = gate[i][:, 128 * n:128 * (n + 1)]
                if n == 0:
                    nc.vector.tensor_tensor(out=pr[:, n, :], in0=src, in1=g, op=ALU.mult)
                else:
                    nc.vector.scalar_tensor_tensor(out=pr[:, n, :], in0=src, scalar=prob(n, j, r), in1=g,
                                                   op0=ALU.mult, op1=ALU.mult)
            prod[i] = pr

        def stage_a(i):
            j, r = divmod(i, 2)
            if r == 0:
                acc[j] = aux([128, 2, 128], "acc")
            for n in range(TOT):
                nc.tensor.matmul(out=acc[j][:, r, :], lhsT=prod[i][:, n, :], rhs=ident[:],
                                 start=(n == 0), stop=(n == TOT - 1), is_transpose=True)

        def stage_f(j):
            o = work.tile([128, 128, 2], F32, name="o", tag="o", bufs=3)
            nc.scalar.copy(out=o[:], in_=acc[j][:].rearrange("c r p -> c p r"))
            nc.sync.dma_start(out=out[:, 256 * j:256 * (j + 1)], in_=o[:].rearrange("c p r -> c (p r)"))

        def ok(i):
            return 0 <= i < 2 * NPAIR

        for g in range(2):
            prep_z(g)
        path_probabilities()
        for i in range(-4, 2 * NPAIR + 1):
            if ok(i):
                stage_m2(i)
            if ok(i + 1):
                stage_e(i + 1)
            if ok(i):
                stage_h(i)
            if ok(i + 2):
                stage_q(i + 2)
            if ok(i + 4):
                stage_p(i + 4)
            if ok(i + 1):
                stage_q2(i + 1)
            if ok(i + 3):
                stage_t(i + 3)
            if ok(i - 1):
                stage_a(i - 1)
            if i == -4:
                prep_w(v_sb, v_codes, v_scales, ((0, 4),))
            if i == -3:
                prep_w(v_sb, v_codes, v_scales, ((4, 2), (6, 1)))
            if i == -2:
                prep_w(w_sb, w_codes, w_scales, ((0, 4),))
            if i == -1:
                prep_w(w_sb, w_codes, w_scales, ((4, 2), (6, 1)))
            if ok(i):
                stage_s(i)
            if ok(i + 3):
                stage_c(i + 3)
            if ok(i - 1) and i % 2 == 0:
                stage_f((i - 1) // 2)
            if ok(i + 2):
                stage_m1(i + 2)
